import numpy as np
import ml_dtypes


def mxq(x, axis, fmt="e4m3"):
    dtype, down = {"e4m3": (ml_dtypes.float8_e4m3fn, 7), "e5m2": (ml_dtypes.float8_e5m2, 14)}[fmt]
    v = np.moveaxis(np.asarray(x, np.float32).astype(ml_dtypes.bfloat16).astype(np.float64), axis, -1)
    blocks = v.reshape(v.shape[:-1] + (-1, 32))
    amax = np.abs(blocks).max(-1, keepdims=True)
    byte = np.maximum(np.where(amax > 0, np.frexp(amax)[1] - 1 + 127, 0) - down, 1)
    scale = np.exp2(byte - 127.0)
    codes = (blocks / scale).astype(np.float32).astype(dtype).astype(np.float64)
    return np.moveaxis((codes * scale).reshape(v.shape), -1, axis)


WIDE = False


def mx_kscale(k):
    if not WIDE:
        return np.ones(k)
    levels = np.array([10, -10, 5, -5, 0])
    a = np.random.permutation(np.resize(levels, k // 512 * 4)).reshape(k // 512, 4)
    idx = np.arange(k)
    return np.exp2(a[idx // 512, idx % 128 // 32])


BF16 = ml_dtypes.bfloat16


def bf(x):
    return np.asarray(x, np.float32).astype(BF16)


def f64(x):
    return np.asarray(x).astype(np.float64)


B, I, H = 512, 256, 1024


def setup_inputs():
    s = mx_kscale(H)
    w1 = np.concatenate([np.random.standard_normal((H, H)) * 1.5 / np.sqrt(H) / s, np.random.standard_normal(H)[:, None] * 0.6], axis=1)
    return {"h_tilde": bf(np.random.standard_normal((B, H)) * 0.3 * s),
            "k_prev": bf(np.random.standard_normal((B, H)) * 0.9 * s),
            "t0": bf(0.2 + 0.1 * np.random.random(1)),
            "t1": bf(1.0 + 0.2 * np.random.random(1)),
            "W1": bf(w1),
            "b1": bf(np.random.standard_normal(H) * 0.3),
            "W2": bf(np.random.standard_normal((H, H)) * 1.5 / np.sqrt(H)),
            "b2": bf(np.random.standard_normal(H) * 0.3)}


def reference(h_tilde, k_prev, t0, t1, W1, b1, W2, b2):
    dt = f64(t1) - f64(t0)
    t = f64(t0) + 0.5 * dt
    y = f64(h_tilde) + 0.5 * dt * f64(k_prev)
    w1 = f64(W1)
    z = np.tanh((mxq(y, 1, "e4m3") @ mxq(w1[:, :H], 1, "e4m3").T) + t * w1[:, H] + f64(b1))
    return (mxq(z, 1, "e4m3") @ mxq(f64(W2), 1, "e4m3").T) + f64(b2)

@@ -1,0 +1,313 @@
+from contextlib import ExitStack
+
+import concourse.mybir as mybir
+from concourse.masks import make_identity
+
+F32 = mybir.dt.float32
+BF16 = mybir.dt.bfloat16
+U32 = mybir.dt.uint32
+U8 = mybir.dt.uint8
+FP8X4 = mybir.dt.float8_e4m3fn_x4
+ALU = mybir.AluOpType
+ACT = mybir.ActivationFunctionType
+
+P = 128
+B = 512
+H = 1024
+PACK = 4
+K_PASS = P * PACK
+PASSES = H // K_PASS
+HALVES = 2
+B_TILES = B // P
+CHUNK_TILES = 2
+CHUNK = CHUNK_TILES * P
+CHUNKS = H // CHUNK
+N_OUT = 512
+OUT_PARTS = H // N_OUT
+W1_PITCH = 1040
+
+FLOPS = 2 * 2 * B * H * H
+
+
+def transpose_rows(nc, bank, words, identity):
+    for g in range(PASSES):
+        for u in range(HALVES):
+            first = (g * HALVES + u) * P
+            nc.tensor.transpose(bank[:, g, u, :], words[:, first : first + P], identity)
+
+
+def by_row(bank):
+    return bank[:].rearrange("p g u r -> p g r u")
+
+
+def tile_nodelstmcell_pb_kernel(tc, h_tilde, k_prev, t0, t1, W1, b1, W2, b2, out):
+    nc = tc.nc
+    with ExitStack() as ctx:
+        sbuf = ctx.enter_context(tc.tile_pool(name="sbuf", bufs=1))
+        flip_psum = ctx.enter_context(tc.psum_pool(name="flip_psum", bufs=4))
+        sum_psum = ctx.enter_context(tc.psum_pool(name="sum_psum", bufs=4))
+        ctx.enter_context(tc.manual_schedule())
+
+        h_view = h_tilde.rearrange("(p t) k -> p t k", t=B_TILES)
+        k_view = k_prev.rearrange("(p t) k -> p t k", t=B_TILES)
+        out_view = out.rearrange("(p t) o -> p t o", t=B_TILES)
+        w1_view = W1.rearrange("(c p e) k -> c p e k", p=P, e=CHUNK_TILES)
+        w2_view = W2.rearrange("(c s p) j -> c p s j", s=CHUNK_TILES, p=P)
+
+        identity = sbuf.tile([P, P], F32, name="identity")
+        make_identity(nc, identity[:])
+        ones = sbuf.tile([P, P], BF16, name="ones")
+        nc.vector.memset(ones[:], 1.0)
+        b1_words = sbuf.tile([P, P], F32, name="b1_words")
+        nc.vector.memset(b1_words[:], 0.0)
+        b2_rows = sbuf.tile([P, H], BF16, name="b2_rows")
+        nc.vector.memset(b2_rows[:], 0.0)
+        zero = sbuf.tile([P, 1], F32, name="zero")
+        nc.vector.memset(zero[:], 0.0)
+
+        t0_all = sbuf.tile([P, 1], BF16, name="t0_all")
+        nc.scalar.dma_start(out=t0_all[:], in_=t0.partition_broadcast(P))
+        t1_all = sbuf.tile([P, 1], BF16, name="t1_all")
+        nc.scalar.dma_start(out=t1_all[:], in_=t1.partition_broadcast(P))
+        nc.scalar.dma_start(
+            out=b1_words[:].bitcast(BF16)[0:CHUNKS, :],
+            in_=b1.rearrange("(c w) -> c w", c=CHUNKS),
+        )
+        nc.scalar.dma_start(out=b2_rows[0:1, :], in_=b2.rearrange("(o n) -> o n", o=1))
+        warm = sbuf.tile([P, 1], F32, name="warm")
+        nc.scalar.activation(out=warm[:], in_=zero[:], func=ACT.Tanh)
+
+        h_rows = []
+        k_rows = []
+        for t in range(B_TILES):
+            h_rows.append(sbuf.tile([P, H], BF16, name="h_rows%d" % t))
+            nc.sync.dma_start(out=h_rows[t][:], in_=h_view[:, t, :])
+            k_rows.append(sbuf.tile([P, H], BF16, name="k_rows%d" % t))
+            nc.sync.dma_start(out=k_rows[t][:], in_=k_view[:, t, :])
+        w1_rows = []
+        for c in range(CHUNKS):
+            w1_rows.append(sbuf.tile([P, CHUNK_TILES, W1_PITCH], BF16, name="w1_rows%d" % c))
+            nc.sync.dma_start(out=w1_rows[c][:, :, 0 : H + 1], in_=w1_view[c])
+        w2_rows = []
+        for c in range(CHUNKS):
+            w2_rows.append(sbuf.tile([P, CHUNK_TILES, H], BF16, name="w2_rows%d" % c))
+            nc.sync.dma_start(out=w2_rows[c][:], in_=w2_view[c])
+
+        step = sbuf.tile([P, 1], F32, name="step")
+        nc.vector.tensor_sub(out=step[:], in0=t1_all[:], in1=t0_all[:])
+        half_step = sbuf.tile([P, 1], F32, name="half_step")
+        nc.vector.tensor_scalar_mul(out=half_step[:], in0=step[:], scalar1=0.5)
+        t_mid = sbuf.tile([P, 1], F32, name="t_mid")
+        nc.vector.tensor_add(out=t_mid[:], in0=t0_all[:], in1=half_step[:])
+
+        b1_bank = flip_psum.tile([P, P], F32, name="b1_bank", tag="bank")
+        nc.tensor.transpose(b1_bank[:], b1_words[:], identity[:])
+        b1_cols = sbuf.tile([P, CHUNKS], F32, name="b1_cols")
+        nc.scalar.copy(out=b1_cols[:], in_=b1_bank[:, 0:CHUNKS])
+        b2_all = []
+        for o in range(OUT_PARTS):
+            b2_bank = flip_psum.tile([P, N_OUT], F32, name="b2_bank", tag="bank")
+            nc.tensor.matmul(
+                out=b2_bank[:],
+                lhsT=ones[:],
+                rhs=b2_rows[:, o * N_OUT : (o + 1) * N_OUT],
+                start=True,
+                stop=True,
+            )
+            b2_all.append(sbuf.tile([P, N_OUT], F32, name="b2_all%d" % o))
+            nc.scalar.copy(out=b2_all[o][:], in_=b2_bank[:])
+
+        y_rows = [sbuf.tile([P, H], BF16, name="y_rows%d" % t) for t in range(B_TILES)]
+        y_grouped = sbuf.tile([P, PASSES, B, PACK], BF16, name="y_grouped", align_bytes=64)
+        y_codes = sbuf.tile([P, PASSES, B], U32, name="y_codes", align_bytes=64)
+        y_scales = sbuf.tile([P, PASSES, B], U8, name="y_scales", align_bytes=64)
+        w1_grouped = []
+        w1_codes = []
+        w1_scales = []
+        w1_bias = []
+        w2_grouped = []
+        for c in range(CHUNKS):
+            w1_grouped.append(
+                sbuf.tile(
+                    [P, CHUNK_TILES, PASSES, P, PACK], BF16, name="w1_grouped%d" % c, align_bytes=64
+                )
+            )
+            w1_codes.append(
+                sbuf.tile([P, CHUNK_TILES, PASSES, P], U32, name="w1_codes%d" % c, align_bytes=64)
+            )
+            w1_scales.append(
+                sbuf.tile([P, CHUNK_TILES, PASSES, P], U8, name="w1_scales%d" % c, align_bytes=64)
+            )
+            w1_bias.append(sbuf.tile([P, CHUNK_TILES], F32, name="w1_bias%d" % c))
+            w2_grouped.append(
+                sbuf.tile([P, PASSES, CHUNK, PACK], BF16, name="w2_grouped%d" % c, align_bytes=64)
+            )
+        z_rows = []
+        z_grouped = []
+        z_codes = []
+        z_scales = []
+        for g in range(PASSES):
+            z_rows.append(sbuf.tile([P, PACK, B], BF16, name="z_rows%d" % g))
+            z_grouped.append(sbuf.tile([P, B, PACK], BF16, name="z_grouped%d" % g, align_bytes=64))
+            z_codes.append(sbuf.tile([P, B], U32, name="z_codes%d" % g, align_bytes=64))
+            z_scales.append(sbuf.tile([P, B], U8, name="z_scales%d" % g, align_bytes=64))
+        w2_codes = []
+        w2_scales = []
+        for o in range(OUT_PARTS):
+            w2_codes.append(sbuf.tile([P, PASSES, N_OUT], U32, name="w2_codes%d" % o, align_bytes=64))
+            w2_scales.append(sbuf.tile([P, PASSES, N_OUT], U8, name="w2_scales%d" % o, align_bytes=64))
+
+        def make_y(t):
+            nc.vector.scalar_tensor_tensor(
+                out=y_rows[t][:],
+                in0=k_rows[t][:],
+                scalar=half_step[:, 0:1],
+                in1=h_rows[t][:],
+                op0=ALU.mult,
+                op1=ALU.add,
+            )
+
+        def flip_y(t):
+            bank = flip_psum.tile([P, PASSES, HALVES, P], F32, name="y_bank", tag="bank")
+            transpose_rows(nc, bank, y_rows[t][:].bitcast(F32), identity[:])
+            nc.scalar.copy(
+                out=y_grouped[:].bitcast(F32)[:, :, t * P : (t + 1) * P, :], in_=by_row(bank)
+            )
+
+        def pack_y(t):
+            cols = slice(t * P, (t + 1) * P)
+            for g in range(PASSES):
+                nc.vector.quantize_mx(
+                    out=y_codes[:, g, cols].bitcast(FP8X4),
+                    scales=y_scales[:, g, cols],
+                    in_=y_grouped[:, g, cols, :].rearrange("p r v -> p (r v)"),
+                )
+
+        def flip_w1(c):
+            for e in range(CHUNK_TILES):
+                bank = flip_psum.tile([P, PASSES, HALVES, P], F32, name="w1_bank", tag="bank")
+                transpose_rows(nc, bank, w1_rows[c][:].bitcast(F32)[:, e, :], identity[:])
+                nc.scalar.copy(out=w1_grouped[c][:].bitcast(F32)[:, e], in_=by_row(bank))
+
+        def pack_w1(c):
+            nc.vector.quantize_mx(
+                out=w1_codes[c][:].rearrange("p e g r -> p (e g r)").bitcast(FP8X4),
+                scales=w1_scales[c][:].rearrange("p e g r -> p (e g r)"),
+                in_=w1_grouped[c][:].rearrange("p e g r v -> p (e g r v)"),
+            )
+            nc.vector.scalar_tensor_tensor(
+                out=w1_bias[c][:],
+                in0=w1_rows[c][:, :, H],
+                scalar=t_mid[:, 0:1],
+                in1=b1_cols[:].bitcast(BF16)[:, c * CHUNK_TILES : (c + 1) * CHUNK_TILES],
+                op0=ALU.mult,
+                op1=ALU.add,
+            )
+
+        def layer_1(c):
+            g_next = c // HALVES
+            u = c % HALVES
+            for e in range(CHUNK_TILES):
+                total = sum_psum.tile([P, B], F32, name="z_total", tag="total")
+                for g in range(PASSES):
+                    nc.tensor.matmul_mx(
+                        out=total[:],
+                        lhsT=w1_codes[c][:, e, g, :].bitcast(FP8X4),
+                        lhsT_scale=w1_scales[c][:, e, g, :],
+                        rhs=y_codes[:, g, :].bitcast(FP8X4),
+                        rhs_scale=y_scales[:, g, :],
+                        start=(g == 0),
+                        stop=(g == PASSES - 1),
+                    )
+                nc.scalar.activation(
+                    out=z_rows[g_next][:, HALVES * u + e, :],
+                    in_=total[:],
+                    func=ACT.Tanh,
+                    bias=w1_bias[c][:, e : e + 1],
+                    scale=1.0,
+                )
+
+        def group_z(g):
+            nc.vector.tensor_copy(
+                out=z_grouped[g][:].rearrange("p (c i) v -> p c v i", i=4),
+                in_=z_rows[g][:].rearrange("p v (c i) -> p c v i", i=4),
+            )
+
+        def pack_z(g):
+            nc.vector.quantize_mx(
+                out=z_codes[g][:].bitcast(FP8X4),
+                scales=z_scales[g][:],
+                in_=z_grouped[g][:].rearrange("p b v -> p (b v)"),
+            )
+
+        def flip_w2(c):
+            for s in range(CHUNK_TILES):
+                bank = flip_psum.tile([P, PASSES, HALVES, P], F32, name="w2_bank", tag="bank")
+                transpose_rows(nc, bank, w2_rows[c][:].bitcast(F32)[:, s, :], identity[:])
+                nc.scalar.copy(
+                    out=w2_grouped[c][:].bitcast(F32)[:, :, s * P : (s + 1) * P, :], in_=by_row(bank)
+                )
+
+        def pack_w2(c):
+            o = c * CHUNK // N_OUT
+            first = c * CHUNK % N_OUT
+            for g in range(PASSES):
+                nc.vector.quantize_mx(
+                    out=w2_codes[o][:, g, first : first + CHUNK].bitcast(FP8X4),
+                    scales=w2_scales[o][:, g, first : first + CHUNK],
+                    in_=w2_grouped[c][:, g].rearrange("p r v -> p (r v)"),
+                )
+
+        def layer_2(o):
+            for t in range(B_TILES):
+                total = sum_psum.tile([P, N_OUT], F32, name="out_total", tag="total")
+                for g in range(PASSES):
+                    nc.tensor.matmul_mx(
+                        out=total[:],
+                        lhsT=z_codes[g][:, t * P : (t + 1) * P].bitcast(FP8X4),
+                        lhsT_scale=z_scales[g][:, t * P : (t + 1) * P],
+                        rhs=w2_codes[o][:, g, :].bitcast(FP8X4),
+                        rhs_scale=w2_scales[o][:, g, :],
+                        start=(g == 0),
+                        stop=(g == PASSES - 1),
+                    )
+                result = sbuf.tile([P, N_OUT], F32, name="result%d_%d" % (o, t))
+                nc.vector.tensor_add(out=result[:], in0=total[:], in1=b2_all[o][:])
+                nc.sync.dma_start(out=out_view[:, t, o * N_OUT : (o + 1) * N_OUT], in_=result[:])
+
+        make_y(0)
+        flip_y(0)
+        make_y(1)
+        flip_y(1)
+        for t in range(2, B_TILES):
+            pack_y(t - 2)
+            make_y(t)
+            flip_y(t)
+        pack_y(B_TILES - 2)
+        flip_w1(0)
+        pack_y(B_TILES - 1)
+        flip_w1(1)
+        pack_w1(0)
+        layer_1(0)
+        flip_w1(2)
+        pack_w1(1)
+        layer_1(1)
+        flip_w1(3)
+        pack_w1(2)
+        group_z(0)
+        layer_1(2)
+        flip_w2(0)
+        pack_w1(3)
+        pack_z(0)
+        layer_1(3)
+        flip_w2(1)
+        pack_w2(0)
+        group_z(1)
+        flip_w2(2)
+        pack_w2(1)
+        pack_z(1)
+        flip_w2(3)
+        pack_w2(2)
+        pack_w2(3)
+        layer_2(0)
+        layer_2(1)

@@ -46,7 +46,6 @@ def tile_nodelstmcell_pb_kernel(tc, h_tilde, k_prev, t0, t1, W1, b1, W2, b2, out
         sbuf = ctx.enter_context(tc.tile_pool(name="sbuf", bufs=1))
         flip_psum = ctx.enter_context(tc.psum_pool(name="flip_psum", bufs=4))
         sum_psum = ctx.enter_context(tc.psum_pool(name="sum_psum", bufs=4))
-        ctx.enter_context(tc.manual_schedule())
 
         h_view = h_tilde.rearrange("(p t) k -> p t k", t=B_TILES)
         k_view = k_prev.rearrange("(p t) k -> p t k", t=B_TILES)

@@ -46,6 +46,7 @@ def tile_nodelstmcell_pb_kernel(tc, h_tilde, k_prev, t0, t1, W1, b1, W2, b2, out
         sbuf = ctx.enter_context(tc.tile_pool(name="sbuf", bufs=1))
         flip_psum = ctx.enter_context(tc.psum_pool(name="flip_psum", bufs=4))
         sum_psum = ctx.enter_context(tc.psum_pool(name="sum_psum", bufs=4))
+        ctx.enter_context(tc.manual_schedule())
 
         h_view = h_tilde.rearrange("(p t) k -> p t k", t=B_TILES)
         k_view = k_prev.rearrange("(p t) k -> p t k", t=B_TILES)
@@ -99,22 +100,25 @@ def tile_nodelstmcell_pb_kernel(tc, h_tilde, k_prev, t0, t1, W1, b1, W2, b2, out
         t_mid = sbuf.tile([P, 1], F32, name="t_mid")
         nc.vector.tensor_add(out=t_mid[:], in0=t0_all[:], in1=half_step[:])
 
-        b1_bank = flip_psum.tile([P, P], F32, name="b1_bank", tag="bank")
-        nc.tensor.transpose(b1_bank[:], b1_words[:], identity[:])
         b1_cols = sbuf.tile([P, CHUNKS], F32, name="b1_cols")
-        nc.scalar.copy(out=b1_cols[:], in_=b1_bank[:, 0:CHUNKS])
-        b2_all = []
-        for o in range(OUT_PARTS):
-            b2_bank = flip_psum.tile([P, N_OUT], F32, name="b2_bank", tag="bank")
-            nc.tensor.matmul(
-                out=b2_bank[:],
-                lhsT=ones[:],
-                rhs=b2_rows[:, o * N_OUT : (o + 1) * N_OUT],
-                start=True,
-                stop=True,
-            )
-            b2_all.append(sbuf.tile([P, N_OUT], F32, name="b2_all%d" % o))
-            nc.scalar.copy(out=b2_all[o][:], in_=b2_bank[:])
+        b2_all = [sbuf.tile([P, N_OUT], F32, name="b2_all%d" % o) for o in range(OUT_PARTS)]
+
+        def spread_b1():
+            b1_bank = flip_psum.tile([P, P], F32, name="b1_bank", tag="bank")
+            nc.tensor.transpose(b1_bank[:], b1_words[:], identity[:])
+            nc.scalar.copy(out=b1_cols[:], in_=b1_bank[:, 0:CHUNKS])
+
+        def spread_b2():
+            for o in range(OUT_PARTS):
+                b2_bank = flip_psum.tile([P, N_OUT], F32, name="b2_bank", tag="bank")
+                nc.tensor.matmul(
+                    out=b2_bank[:],
+                    lhsT=ones[:],
+                    rhs=b2_rows[:, o * N_OUT : (o + 1) * N_OUT],
+                    start=True,
+                    stop=True,
+                )
+                nc.scalar.copy(out=b2_all[o][:], in_=b2_bank[:])
 
         y_rows = [sbuf.tile([P, H], BF16, name="y_rows%d" % t) for t in range(B_TILES)]
         y_grouped = sbuf.tile([P, PASSES, B, PACK], BF16, name="y_grouped", align_bytes=64)
@@ -186,7 +190,11 @@ def tile_nodelstmcell_pb_kernel(tc, h_tilde, k_prev, t0, t1, W1, b1, W2, b2, out
             for e in range(CHUNK_TILES):
                 bank = flip_psum.tile([P, PASSES, HALVES, P], F32, name="w1_bank", tag="bank")
                 transpose_rows(nc, bank, w1_rows[c][:].bitcast(F32)[:, e, :], identity[:])
-                nc.scalar.copy(out=w1_grouped[c][:].bitcast(F32)[:, e], in_=by_row(bank))
+                grouped_words = w1_grouped[c][:].bitcast(F32)[:, e]
+                if e == 0:
+                    nc.scalar.copy(out=grouped_words, in_=by_row(bank))
+                else:
+                    nc.vector.tensor_copy(out=grouped_words, in_=by_row(bank))
 
         def pack_w1(c):
             nc.vector.quantize_mx(
@@ -276,35 +284,37 @@ def tile_nodelstmcell_pb_kernel(tc, h_tilde, k_prev, t0, t1, W1, b1, W2, b2, out
 
         make_y(0)
         flip_y(0)
+        spread_b1()
         make_y(1)
         flip_y(1)
-        for t in range(2, B_TILES):
-            pack_y(t - 2)
-            make_y(t)
-            flip_y(t)
-        pack_y(B_TILES - 2)
+        spread_b2()
+        make_y(2)
+        flip_y(2)
+        pack_y(0)
+        make_y(3)
+        pack_y(1)
         flip_w1(0)
-        pack_y(B_TILES - 1)
+        flip_y(3)
+        pack_y(2)
         flip_w1(1)
+        pack_y(3)
         pack_w1(0)
-        layer_1(0)
         flip_w1(2)
         pack_w1(1)
-        layer_1(1)
         flip_w1(3)
         pack_w1(2)
-        group_z(0)
-        layer_1(2)
-        flip_w2(0)
         pack_w1(3)
+        for c in range(CHUNKS):
+            layer_1(c)
+        group_z(0)
         pack_z(0)
-        layer_1(3)
+        flip_w2(0)
         flip_w2(1)
-        pack_w2(0)
         group_z(1)
+        pack_w2(0)
+        pack_z(1)
         flip_w2(2)
         pack_w2(1)
-        pack_z(1)
         flip_w2(3)
         pack_w2(2)
         pack_w2(3)

@@ -251,9 +251,11 @@ def tile_nodelstmcell_pb_kernel(tc, h_tilde, k_prev, t0, t1, W1, b1, W2, b2, out
             for s in range(CHUNK_TILES):
                 bank = flip_psum.tile([P, PASSES, HALVES, P], F32, name="w2_bank", tag="bank")
                 transpose_rows(nc, bank, w2_rows[c][:].bitcast(F32)[:, s, :], identity[:])
-                nc.scalar.copy(
-                    out=w2_grouped[c][:].bitcast(F32)[:, :, s * P : (s + 1) * P, :], in_=by_row(bank)
-                )
+                grouped_words = w2_grouped[c][:].bitcast(F32)[:, :, s * P : (s + 1) * P, :]
+                if c * CHUNK < N_OUT:
+                    nc.vector.tensor_copy(out=grouped_words, in_=by_row(bank))
+                else:
+                    nc.scalar.copy(out=grouped_words, in_=by_row(bank))
 
         def pack_w2(c):
             o = c * CHUNK // N_OUT
@@ -265,58 +267,70 @@ def tile_nodelstmcell_pb_kernel(tc, h_tilde, k_prev, t0, t1, W1, b1, W2, b2, out
                     in_=w2_grouped[c][:, g].rearrange("p r v -> p (r v)"),
                 )
 
-        def layer_2(o):
-            for t in range(B_TILES):
-                total = sum_psum.tile([P, N_OUT], F32, name="out_total", tag="total")
-                for g in range(PASSES):
-                    nc.tensor.matmul_mx(
-                        out=total[:],
-                        lhsT=z_codes[g][:, t * P : (t + 1) * P].bitcast(FP8X4),
-                        lhsT_scale=z_scales[g][:, t * P : (t + 1) * P],
-                        rhs=w2_codes[o][:, g, :].bitcast(FP8X4),
-                        rhs_scale=w2_scales[o][:, g, :],
-                        start=(g == 0),
-                        stop=(g == PASSES - 1),
-                    )
-                result = sbuf.tile([P, N_OUT], F32, name="result%d_%d" % (o, t))
-                nc.vector.tensor_add(out=result[:], in0=total[:], in1=b2_all[o][:])
-                nc.sync.dma_start(out=out_view[:, t, o * N_OUT : (o + 1) * N_OUT], in_=result[:])
+        def layer_2_pass(total, o, t, g):
+            nc.tensor.matmul_mx(
+                out=total[:],
+                lhsT=z_codes[g][:, t * P : (t + 1) * P].bitcast(FP8X4),
+                lhsT_scale=z_scales[g][:, t * P : (t + 1) * P],
+                rhs=w2_codes[o][:, g, :].bitcast(FP8X4),
+                rhs_scale=w2_scales[o][:, g, :],
+                start=(g == 0),
+                stop=(g == PASSES - 1),
+            )
+
+        def new_total():
+            return sum_psum.tile([P, N_OUT], F32, name="out_total", tag="total")
+
+        def finish(total, o, t):
+            result = sbuf.tile([P, N_OUT], F32, name="result%d_%d" % (o, t))
+            nc.vector.tensor_add(out=result[:], in0=total[:], in1=b2_all[o][:])
+            nc.sync.dma_start(out=out_view[:, t, o * N_OUT : (o + 1) * N_OUT], in_=result[:])
 
         make_y(0)
         flip_y(0)
-        spread_b1()
         make_y(1)
         flip_y(1)
         spread_b2()
         make_y(2)
         flip_y(2)
-        pack_y(0)
+        spread_b1()
         make_y(3)
+        pack_y(0)
         pack_y(1)
         flip_w1(0)
         flip_y(3)
         pack_y(2)
         flip_w1(1)
-        pack_y(3)
         pack_w1(0)
+        pack_y(3)
         flip_w1(2)
         pack_w1(1)
         flip_w1(3)
         pack_w1(2)
         pack_w1(3)
-        for c in range(CHUNKS):
-            layer_1(c)
-        group_z(0)
-        pack_z(0)
+        layer_1(0)
         flip_w2(0)
         flip_w2(1)
-        group_z(1)
+        for c in range(1, CHUNKS):
+            layer_1(c)
         pack_w2(0)
-        pack_z(1)
-        flip_w2(2)
+        group_z(0)
         pack_w2(1)
+        pack_z(0)
+        flip_w2(2)
         flip_w2(3)
+        first_range = [new_total() for t in range(B_TILES)]
+        for t in range(B_TILES):
+            layer_2_pass(first_range[t], 0, t, 0)
+        group_z(1)
+        pack_z(1)
         pack_w2(2)
         pack_w2(3)
-        layer_2(0)
-        layer_2(1)
+        for t in range(B_TILES):
+            layer_2_pass(first_range[t], 0, t, 1)
+            finish(first_range[t], 0, t)
+        for t in range(B_TILES):
+            total = new_total()
+            for g in range(PASSES):
+                layer_2_pass(total, 1, t, g)
+            finish(total, 1, t)

@@ -24,6 +24,7 @@ CHUNK = CHUNK_TILES * P
 CHUNKS = H // CHUNK
 N_OUT = 512
 OUT_PARTS = H // N_OUT
+B_HALVES = (slice(0, B // 2), slice(B // 2, B))
 W1_PITCH = 1040
 
 FLOPS = 2 * 2 * B * H * H
@@ -56,12 +57,8 @@ def tile_nodelstmcell_pb_kernel(tc, h_tilde, k_prev, t0, t1, W1, b1, W2, b2, out
 
         identity = sbuf.tile([P, P], F32, name="identity")
         make_identity(nc, identity[:])
-        ones = sbuf.tile([P, P], BF16, name="ones")
-        nc.vector.memset(ones[:], 1.0)
         b1_words = sbuf.tile([P, P], F32, name="b1_words")
         nc.vector.memset(b1_words[:], 0.0)
-        b2_rows = sbuf.tile([P, H], BF16, name="b2_rows")
-        nc.vector.memset(b2_rows[:], 0.0)
         zero = sbuf.tile([P, 1], F32, name="zero")
         nc.vector.memset(zero[:], 0.0)
 
@@ -73,7 +70,6 @@ def tile_nodelstmcell_pb_kernel(tc, h_tilde, k_prev, t0, t1, W1, b1, W2, b2, out
             out=b1_words[:].bitcast(BF16)[0:CHUNKS, :],
             in_=b1.rearrange("(c w) -> c w", c=CHUNKS),
         )
-        nc.scalar.dma_start(out=b2_rows[0:1, :], in_=b2.rearrange("(o n) -> o n", o=1))
         warm = sbuf.tile([P, 1], F32, name="warm")
         nc.scalar.activation(out=warm[:], in_=zero[:], func=ACT.Tanh)
 
@@ -92,6 +88,8 @@ def tile_nodelstmcell_pb_kernel(tc, h_tilde, k_prev, t0, t1, W1, b1, W2, b2, out
         for c in range(CHUNKS):
             w2_rows.append(sbuf.tile([P, CHUNK_TILES, H], BF16, name="w2_rows%d" % c))
             nc.sync.dma_start(out=w2_rows[c][:], in_=w2_view[c])
+        b2_all = sbuf.tile([P, H], BF16, name="b2_all")
+        nc.sync.dma_start(out=b2_all[:], in_=b2.partition_broadcast(P))
 
         step = sbuf.tile([P, 1], F32, name="step")
         nc.vector.tensor_sub(out=step[:], in0=t1_all[:], in1=t0_all[:])
@@ -101,24 +99,11 @@ def tile_nodelstmcell_pb_kernel(tc, h_tilde, k_prev, t0, t1, W1, b1, W2, b2, out
         nc.vector.tensor_add(out=t_mid[:], in0=t0_all[:], in1=half_step[:])
 
         b1_cols = sbuf.tile([P, CHUNKS], F32, name="b1_cols")
-        b2_all = [sbuf.tile([P, N_OUT], F32, name="b2_all%d" % o) for o in range(OUT_PARTS)]
 
         def spread_b1():
             b1_bank = flip_psum.tile([P, P], F32, name="b1_bank", tag="bank")
             nc.tensor.transpose(b1_bank[:], b1_words[:], identity[:])
             nc.scalar.copy(out=b1_cols[:], in_=b1_bank[:, 0:CHUNKS])
-
-        def spread_b2():
-            for o in range(OUT_PARTS):
-                b2_bank = flip_psum.tile([P, N_OUT], F32, name="b2_bank", tag="bank")
-                nc.tensor.matmul(
-                    out=b2_bank[:],
-                    lhsT=ones[:],
-                    rhs=b2_rows[:, o * N_OUT : (o + 1) * N_OUT],
-                    start=True,
-                    stop=True,
-                )
-                nc.scalar.copy(out=b2_all[o][:], in_=b2_bank[:])
 
         y_rows = [sbuf.tile([P, H], BF16, name="y_rows%d" % t) for t in range(B_TILES)]
         y_grouped = sbuf.tile([P, PASSES, B, PACK], BF16, name="y_grouped", align_bytes=64)
@@ -235,17 +220,19 @@ def tile_nodelstmcell_pb_kernel(tc, h_tilde, k_prev, t0, t1, W1, b1, W2, b2, out
                 )
 
         def group_z(g):
-            nc.vector.tensor_copy(
-                out=z_grouped[g][:].rearrange("p (c i) v -> p c v i", i=4),
-                in_=z_rows[g][:].rearrange("p v (c i) -> p c v i", i=4),
-            )
+            for cols in B_HALVES:
+                nc.vector.tensor_copy(
+                    out=z_grouped[g][:, cols, :].rearrange("p (c i) v -> p c v i", i=4),
+                    in_=z_rows[g][:, :, cols].rearrange("p v (c i) -> p c v i", i=4),
+                )
 
         def pack_z(g):
-            nc.vector.quantize_mx(
-                out=z_codes[g][:].bitcast(FP8X4),
-                scales=z_scales[g][:],
-                in_=z_grouped[g][:].rearrange("p b v -> p (b v)"),
-            )
+            for cols in B_HALVES:
+                nc.vector.quantize_mx(
+                    out=z_codes[g][:, cols].bitcast(FP8X4),
+                    scales=z_scales[g][:, cols],
+                    in_=z_grouped[g][:, cols, :].rearrange("p b v -> p (b v)"),
+                )
 
         def flip_w2(c):
             for s in range(CHUNK_TILES):
@@ -283,14 +270,15 @@ def tile_nodelstmcell_pb_kernel(tc, h_tilde, k_prev, t0, t1, W1, b1, W2, b2, out
 
         def finish(total, o, t):
             result = sbuf.tile([P, N_OUT], F32, name="result%d_%d" % (o, t))
-            nc.vector.tensor_add(out=result[:], in0=total[:], in1=b2_all[o][:])
+            nc.vector.tensor_add(
+                out=result[:], in0=total[:], in1=b2_all[:, o * N_OUT : (o + 1) * N_OUT]
+            )
             nc.sync.dma_start(out=out_view[:, t, o * N_OUT : (o + 1) * N_OUT], in_=result[:])
 
         make_y(0)
         flip_y(0)
         make_y(1)
         flip_y(1)
-        spread_b2()
         make_y(2)
         flip_y(2)
         spread_b1()

@@ -239,7 +239,7 @@ def tile_nodelstmcell_pb_kernel(tc, h_tilde, k_prev, t0, t1, W1, b1, W2, b2, out
                 bank = flip_psum.tile([P, PASSES, HALVES, P], F32, name="w2_bank", tag="bank")
                 transpose_rows(nc, bank, w2_rows[c][:].bitcast(F32)[:, s, :], identity[:])
                 grouped_words = w2_grouped[c][:].bitcast(F32)[:, :, s * P : (s + 1) * P, :]
-                if c * CHUNK < N_OUT:
+                if c * CHUNK < N_OUT and s == 1:
                     nc.vector.tensor_copy(out=grouped_words, in_=by_row(bank))
                 else:
                     nc.scalar.copy(out=grouped_words, in_=by_row(bank))

@@ -70,6 +70,8 @@ def tile_nodelstmcell_pb_kernel(tc, h_tilde, k_prev, t0, t1, W1, b1, W2, b2, out
             out=b1_words[:].bitcast(BF16)[0:CHUNKS, :],
             in_=b1.rearrange("(c w) -> c w", c=CHUNKS),
         )
+        blank = sbuf.tile([P, N_OUT], BF16, name="blank")
+        nc.vector.memset(blank[:], 0.0)
         warm = sbuf.tile([P, 1], F32, name="warm")
         nc.scalar.activation(out=warm[:], in_=zero[:], func=ACT.Tanh)
 
@@ -275,23 +277,37 @@ def tile_nodelstmcell_pb_kernel(tc, h_tilde, k_prev, t0, t1, W1, b1, W2, b2, out
             )
             nc.sync.dma_start(out=out_view[:, t, o * N_OUT : (o + 1) * N_OUT], in_=result[:])
 
+        def keep_clock(rows):
+            unread = sum_psum.tile([P, N_OUT], F32, name="unread", tag="total")
+            nc.tensor.matmul(unread[:], lhsT=blank[:, 0:P], rhs=rows, start=True, stop=True)
+
+        for i in range(4):
+            keep_clock(blank[:])
+        keep_clock(h_rows[0][:, 0:N_OUT])
+        keep_clock(h_rows[0][:, N_OUT:H])
         make_y(0)
         flip_y(0)
+        keep_clock(h_rows[1][:, 0:N_OUT])
         make_y(1)
         flip_y(1)
+        keep_clock(h_rows[2][:, 0:N_OUT])
         make_y(2)
         flip_y(2)
         spread_b1()
+        keep_clock(h_rows[3][:, 0:N_OUT])
         make_y(3)
         pack_y(0)
         pack_y(1)
         flip_w1(0)
         flip_y(3)
+        keep_clock(blank[:])
         pack_y(2)
         flip_w1(1)
+        keep_clock(blank[:])
         pack_w1(0)
         pack_y(3)
         flip_w1(2)
+        keep_clock(blank[:])
         pack_w1(1)
         flip_w1(3)
         pack_w1(2)

@@ -41,6 +41,12 @@ def by_row(bank):
     return bank[:].rearrange("p g u r -> p g r u")
 
 
+def y_parts(t):
+    parts = 2 if t == 0 else 1
+    width = H // parts
+    return [slice(i * width, (i + 1) * width) for i in range(parts)]
+
+
 def tile_nodelstmcell_pb_kernel(tc, h_tilde, k_prev, t0, t1, W1, b1, W2, b2, out):
     nc = tc.nc
     with ExitStack() as ctx:
@@ -66,10 +72,6 @@ def tile_nodelstmcell_pb_kernel(tc, h_tilde, k_prev, t0, t1, W1, b1, W2, b2, out
         nc.scalar.dma_start(out=t0_all[:], in_=t0.partition_broadcast(P))
         t1_all = sbuf.tile([P, 1], BF16, name="t1_all")
         nc.scalar.dma_start(out=t1_all[:], in_=t1.partition_broadcast(P))
-        nc.scalar.dma_start(
-            out=b1_words[:].bitcast(BF16)[0:CHUNKS, :],
-            in_=b1.rearrange("(c w) -> c w", c=CHUNKS),
-        )
         blank = sbuf.tile([P, N_OUT], BF16, name="blank")
         nc.vector.memset(blank[:], 0.0)
         warm = sbuf.tile([P, 1], F32, name="warm")
@@ -79,9 +81,14 @@ def tile_nodelstmcell_pb_kernel(tc, h_tilde, k_prev, t0, t1, W1, b1, W2, b2, out
         k_rows = []
         for t in range(B_TILES):
             h_rows.append(sbuf.tile([P, H], BF16, name="h_rows%d" % t))
-            nc.sync.dma_start(out=h_rows[t][:], in_=h_view[:, t, :])
             k_rows.append(sbuf.tile([P, H], BF16, name="k_rows%d" % t))
-            nc.sync.dma_start(out=k_rows[t][:], in_=k_view[:, t, :])
+            for cols in y_parts(t):
+                nc.sync.dma_start(out=h_rows[t][:, cols], in_=h_view[:, t, cols])
+                nc.sync.dma_start(out=k_rows[t][:, cols], in_=k_view[:, t, cols])
+        nc.sync.dma_start(
+            out=b1_words[:].bitcast(BF16)[0:CHUNKS, :],
+            in_=b1.rearrange("(c w) -> c w", c=CHUNKS),
+        )
         w1_rows = []
         for c in range(CHUNKS):
             w1_rows.append(sbuf.tile([P, CHUNK_TILES, W1_PITCH], BF16, name="w1_rows%d" % c))
@@ -93,10 +100,15 @@ def tile_nodelstmcell_pb_kernel(tc, h_tilde, k_prev, t0, t1, W1, b1, W2, b2, out
         b2_all = sbuf.tile([P, H], BF16, name="b2_all")
         nc.sync.dma_start(out=b2_all[:], in_=b2.partition_broadcast(P))
 
-        step = sbuf.tile([P, 1], F32, name="step")
-        nc.vector.tensor_sub(out=step[:], in0=t1_all[:], in1=t0_all[:])
         half_step = sbuf.tile([P, 1], F32, name="half_step")
-        nc.vector.tensor_scalar_mul(out=half_step[:], in0=step[:], scalar1=0.5)
+        nc.vector.tensor_scalar(
+            out=half_step[:],
+            in0=t1_all[:],
+            scalar1=t0_all[:, 0:1],
+            scalar2=0.5,
+            op0=ALU.subtract,
+            op1=ALU.mult,
+        )
         t_mid = sbuf.tile([P, 1], F32, name="t_mid")
         nc.vector.tensor_add(out=t_mid[:], in0=t0_all[:], in1=half_step[:])
 
@@ -148,14 +160,15 @@ def tile_nodelstmcell_pb_kernel(tc, h_tilde, k_prev, t0, t1, W1, b1, W2, b2, out
             w2_scales.append(sbuf.tile([P, PASSES, N_OUT], U8, name="w2_scales%d" % o, align_bytes=64))
 
         def make_y(t):
-            nc.vector.scalar_tensor_tensor(
-                out=y_rows[t][:],
-                in0=k_rows[t][:],
-                scalar=half_step[:, 0:1],
-                in1=h_rows[t][:],
-                op0=ALU.mult,
-                op1=ALU.add,
-            )
+            for cols in y_parts(t):
+                nc.vector.scalar_tensor_tensor(
+                    out=y_rows[t][:, cols],
+                    in0=k_rows[t][:, cols],
+                    scalar=half_step[:, 0:1],
+                    in1=h_rows[t][:, cols],
+                    op0=ALU.mult,
+                    op1=ALU.add,
+                )
 
         def flip_y(t):
             bank = flip_psum.tile([P, PASSES, HALVES, P], F32, name="y_bank", tag="bank")

@@ -191,7 +191,7 @@ def tile_nodelstmcell_pb_kernel(tc, h_tilde, k_prev, t0, t1, W1, b1, W2, b2, out
                 bank = flip_psum.tile([P, PASSES, HALVES, P], F32, name="w1_bank", tag="bank")
                 transpose_rows(nc, bank, w1_rows[c][:].bitcast(F32)[:, e, :], identity[:])
                 grouped_words = w1_grouped[c][:].bitcast(F32)[:, e]
-                if e == 0:
+                if e == 0 or c == 2:
                     nc.scalar.copy(out=grouped_words, in_=by_row(bank))
                 else:
                     nc.vector.tensor_copy(out=grouped_words, in_=by_row(bank))

from contextlib import ExitStack

import concourse.mybir as mybir
from concourse.masks import make_identity

F32 = mybir.dt.float32
BF16 = mybir.dt.bfloat16
U32 = mybir.dt.uint32
U8 = mybir.dt.uint8
FP8X4 = mybir.dt.float8_e4m3fn_x4
ALU = mybir.AluOpType
ACT = mybir.ActivationFunctionType

P = 128
B = 512
H = 1024
PACK = 4
K_PASS = P * PACK
PASSES = H // K_PASS
HALVES = 2
B_TILES = B // P
CHUNK_TILES = 2
CHUNK = CHUNK_TILES * P
CHUNKS = H // CHUNK
N_OUT = 512
OUT_PARTS = H // N_OUT
B_HALVES = (slice(0, B // 2), slice(B // 2, B))
W1_PITCH = 1040

FLOPS = 2 * 2 * B * H * H


def transpose_rows(nc, bank, words, identity):
    for g in range(PASSES):
        for u in range(HALVES):
            first = (g * HALVES + u) * P
            nc.tensor.transpose(bank[:, g, u, :], words[:, first : first + P], identity)


def by_row(bank):
    return bank[:].rearrange("p g u r -> p g r u")


def y_parts(t):
    parts = 2 if t == 0 else 1
    width = H // parts
    return [slice(i * width, (i + 1) * width) for i in range(parts)]


def tile_nodelstmcell_pb_kernel(tc, h_tilde, k_prev, t0, t1, W1, b1, W2, b2, out):
    nc = tc.nc
    with ExitStack() as ctx:
        sbuf = ctx.enter_context(tc.tile_pool(name="sbuf", bufs=1))
        flip_psum = ctx.enter_context(tc.psum_pool(name="flip_psum", bufs=4))
        sum_psum = ctx.enter_context(tc.psum_pool(name="sum_psum", bufs=4))
        ctx.enter_context(tc.manual_schedule())

        h_view = h_tilde.rearrange("(p t) k -> p t k", t=B_TILES)
        k_view = k_prev.rearrange("(p t) k -> p t k", t=B_TILES)
        out_view = out.rearrange("(p t) o -> p t o", t=B_TILES)
        w1_view = W1.rearrange("(c p e) k -> c p e k", p=P, e=CHUNK_TILES)
        w2_view = W2.rearrange("(c s p) j -> c p s j", s=CHUNK_TILES, p=P)

        identity = sbuf.tile([P, P], F32, name="identity")
        make_identity(nc, identity[:])
        b1_words = sbuf.tile([P, P], F32, name="b1_words")
        nc.vector.memset(b1_words[:], 0.0)
        zero = sbuf.tile([P, 1], F32, name="zero")
        nc.vector.memset(zero[:], 0.0)

        t0_all = sbuf.tile([P, 1], BF16, name="t0_all")
        nc.scalar.dma_start(out=t0_all[:], in_=t0.partition_broadcast(P))
        t1_all = sbuf.tile([P, 1], BF16, name="t1_all")
        nc.scalar.dma_start(out=t1_all[:], in_=t1.partition_broadcast(P))
        blank = sbuf.tile([P, N_OUT], BF16, name="blank")
        nc.vector.memset(blank[:], 0.0)
        warm = sbuf.tile([P, 1], F32, name="warm")
        nc.scalar.activation(out=warm[:], in_=zero[:], func=ACT.Tanh)

        h_rows = []
        k_rows = []
        for t in range(B_TILES):
            h_rows.append(sbuf.tile([P, H], BF16, name="h_rows%d" % t))
            k_rows.append(sbuf.tile([P, H], BF16, name="k_rows%d" % t))
            for cols in y_parts(t):
                nc.sync.dma_start(out=h_rows[t][:, cols], in_=h_view[:, t, cols])
                nc.sync.dma_start(out=k_rows[t][:, cols], in_=k_view[:, t, cols])
        nc.sync.dma_start(
            out=b1_words[:].bitcast(BF16)[0:CHUNKS, :],
            in_=b1.rearrange("(c w) -> c w", c=CHUNKS),
        )
        w1_rows = []
        for c in range(CHUNKS):
            w1_rows.append(sbuf.tile([P, CHUNK_TILES, W1_PITCH], BF16, name="w1_rows%d" % c))
            nc.sync.dma_start(out=w1_rows[c][:, :, 0 : H + 1], in_=w1_view[c])
        w2_rows = []
        for c in range(CHUNKS):
            w2_rows.append(sbuf.tile([P, CHUNK_TILES, H], BF16, name="w2_rows%d" % c))
            nc.sync.dma_start(out=w2_rows[c][:], in_=w2_view[c])
        b2_all = sbuf.tile([P, H], BF16, name="b2_all")
        nc.sync.dma_start(out=b2_all[:], in_=b2.partition_broadcast(P))

        half_step = sbuf.tile([P, 1], F32, name="half_step")
        nc.vector.tensor_scalar(
            out=half_step[:],
            in0=t1_all[:],
            scalar1=t0_all[:, 0:1],
            scalar2=0.5,
            op0=ALU.subtract,
            op1=ALU.mult,
        )
        t_mid = sbuf.tile([P, 1], F32, name="t_mid")
        nc.vector.tensor_add(out=t_mid[:], in0=t0_all[:], in1=half_step[:])

        b1_cols = sbuf.tile([P, CHUNKS], F32, name="b1_cols")

        def spread_b1():
            b1_bank = flip_psum.tile([P, P], F32, name="b1_bank", tag="bank")
            nc.tensor.transpose(b1_bank[:], b1_words[:], identity[:])
            nc.scalar.copy(out=b1_cols[:], in_=b1_bank[:, 0:CHUNKS])

        y_rows = [sbuf.tile([P, H], BF16, name="y_rows%d" % t) for t in range(B_TILES)]
        y_grouped = sbuf.tile([P, PASSES, B, PACK], BF16, name="y_grouped", align_bytes=64)
        y_codes = sbuf.tile([P, PASSES, B], U32, name="y_codes", align_bytes=64)
        y_scales = sbuf.tile([P, PASSES, B], U8, name="y_scales", align_bytes=64)
        w1_grouped = []
        w1_codes = []
        w1_scales = []
        w1_bias = []
        w2_grouped = []
        for c in range(CHUNKS):
            w1_grouped.append(
                sbuf.tile(
                    [P, CHUNK_TILES, PASSES, P, PACK], BF16, name="w1_grouped%d" % c, align_bytes=64
                )
            )
            w1_codes.append(
                sbuf.tile([P, CHUNK_TILES, PASSES, P], U32, name="w1_codes%d" % c, align_bytes=64)
            )
            w1_scales.append(
                sbuf.tile([P, CHUNK_TILES, PASSES, P], U8, name="w1_scales%d" % c, align_bytes=64)
            )
            w1_bias.append(sbuf.tile([P, CHUNK_TILES], F32, name="w1_bias%d" % c))
            w2_grouped.append(
                sbuf.tile([P, PASSES, CHUNK, PACK], BF16, name="w2_grouped%d" % c, align_bytes=64)
            )
        z_rows = []
        z_grouped = []
        z_codes = []
        z_scales = []
        for g in range(PASSES):
            z_rows.append(sbuf.tile([P, PACK, B], BF16, name="z_rows%d" % g))
            z_grouped.append(sbuf.tile([P, B, PACK], BF16, name="z_grouped%d" % g, align_bytes=64))
            z_codes.append(sbuf.tile([P, B], U32, name="z_codes%d" % g, align_bytes=64))
            z_scales.append(sbuf.tile([P, B], U8, name="z_scales%d" % g, align_bytes=64))
        w2_codes = []
        w2_scales = []
        for o in range(OUT_PARTS):
            w2_codes.append(sbuf.tile([P, PASSES, N_OUT], U32, name="w2_codes%d" % o, align_bytes=64))
            w2_scales.append(sbuf.tile([P, PASSES, N_OUT], U8, name="w2_scales%d" % o, align_bytes=64))

        def make_y(t):
            for cols in y_parts(t):
                nc.vector.scalar_tensor_tensor(
                    out=y_rows[t][:, cols],
                    in0=k_rows[t][:, cols],
                    scalar=half_step[:, 0:1],
                    in1=h_rows[t][:, cols],
                    op0=ALU.mult,
                    op1=ALU.add,
                )

        def flip_y(t):
            bank = flip_psum.tile([P, PASSES, HALVES, P], F32, name="y_bank", tag="bank")
            transpose_rows(nc, bank, y_rows[t][:].bitcast(F32), identity[:])
            nc.scalar.copy(
                out=y_grouped[:].bitcast(F32)[:, :, t * P : (t + 1) * P, :], in_=by_row(bank)
            )

        def pack_y(t):
            cols = slice(t * P, (t + 1) * P)
            for g in range(PASSES):
                nc.vector.quantize_mx(
                    out=y_codes[:, g, cols].bitcast(FP8X4),
                    scales=y_scales[:, g, cols],
                    in_=y_grouped[:, g, cols, :].rearrange("p r v -> p (r v)"),
                )

        def flip_w1(c):
            for e in range(CHUNK_TILES):
                bank = flip_psum.tile([P, PASSES, HALVES, P], F32, name="w1_bank", tag="bank")
                transpose_rows(nc, bank, w1_rows[c][:].bitcast(F32)[:, e, :], identity[:])
                grouped_words = w1_grouped[c][:].bitcast(F32)[:, e]
                if e == 0 or c == 2:
                    nc.scalar.copy(out=grouped_words, in_=by_row(bank))
                else:
                    nc.vector.tensor_copy(out=grouped_words, in_=by_row(bank))

        def pack_w1(c):
            nc.vector.quantize_mx(
                out=w1_codes[c][:].rearrange("p e g r -> p (e g r)").bitcast(FP8X4),
                scales=w1_scales[c][:].rearrange("p e g r -> p (e g r)"),
                in_=w1_grouped[c][:].rearrange("p e g r v -> p (e g r v)"),
            )
            nc.vector.scalar_tensor_tensor(
                out=w1_bias[c][:],
                in0=w1_rows[c][:, :, H],
                scalar=t_mid[:, 0:1],
                in1=b1_cols[:].bitcast(BF16)[:, c * CHUNK_TILES : (c + 1) * CHUNK_TILES],
                op0=ALU.mult,
                op1=ALU.add,
            )

        def layer_1(c):
            g_next = c // HALVES
            u = c % HALVES
            for e in range(CHUNK_TILES):
                total = sum_psum.tile([P, B], F32, name="z_total", tag="total")
                for g in range(PASSES):
                    nc.tensor.matmul_mx(
                        out=total[:],
                        lhsT=w1_codes[c][:, e, g, :].bitcast(FP8X4),
                        lhsT_scale=w1_scales[c][:, e, g, :],
                        rhs=y_codes[:, g, :].bitcast(FP8X4),
                        rhs_scale=y_scales[:, g, :],
                        start=(g == 0),
                        stop=(g == PASSES - 1),
                    )
                nc.scalar.activation(
                    out=z_rows[g_next][:, HALVES * u + e, :],
                    in_=total[:],
                    func=ACT.Tanh,
                    bias=w1_bias[c][:, e : e + 1],
                    scale=1.0,
                )

        def group_z(g):
            for cols in B_HALVES:
                nc.vector.tensor_copy(
                    out=z_grouped[g][:, cols, :].rearrange("p (c i) v -> p c v i", i=4),
                    in_=z_rows[g][:, :, cols].rearrange("p v (c i) -> p c v i", i=4),
                )

        def pack_z(g):
            for cols in B_HALVES:
                nc.vector.quantize_mx(
                    out=z_codes[g][:, cols].bitcast(FP8X4),
                    scales=z_scales[g][:, cols],
                    in_=z_grouped[g][:, cols, :].rearrange("p b v -> p (b v)"),
                )

        def flip_w2(c):
            for s in range(CHUNK_TILES):
                bank = flip_psum.tile([P, PASSES, HALVES, P], F32, name="w2_bank", tag="bank")
                transpose_rows(nc, bank, w2_rows[c][:].bitcast(F32)[:, s, :], identity[:])
                grouped_words = w2_grouped[c][:].bitcast(F32)[:, :, s * P : (s + 1) * P, :]
                if c * CHUNK < N_OUT and s == 1:
                    nc.vector.tensor_copy(out=grouped_words, in_=by_row(bank))
                else:
                    nc.scalar.copy(out=grouped_words, in_=by_row(bank))

        def pack_w2(c):
            o = c * CHUNK // N_OUT
            first = c * CHUNK % N_OUT
            for g in range(PASSES):
                nc.vector.quantize_mx(
                    out=w2_codes[o][:, g, first : first + CHUNK].bitcast(FP8X4),
                    scales=w2_scales[o][:, g, first : first + CHUNK],
                    in_=w2_grouped[c][:, g].rearrange("p r v -> p (r v)"),
                )

        def layer_2_pass(total, o, t, g):
            nc.tensor.matmul_mx(
                out=total[:],
                lhsT=z_codes[g][:, t * P : (t + 1) * P].bitcast(FP8X4),
                lhsT_scale=z_scales[g][:, t * P : (t + 1) * P],
                rhs=w2_codes[o][:, g, :].bitcast(FP8X4),
                rhs_scale=w2_scales[o][:, g, :],
                start=(g == 0),
                stop=(g == PASSES - 1),
            )

        def new_total():
            return sum_psum.tile([P, N_OUT], F32, name="out_total", tag="total")

        def finish(total, o, t):
            result = sbuf.tile([P, N_OUT], F32, name="result%d_%d" % (o, t))
            nc.vector.tensor_add(
                out=result[:], in0=total[:], in1=b2_all[:, o * N_OUT : (o + 1) * N_OUT]
            )
            nc.sync.dma_start(out=out_view[:, t, o * N_OUT : (o + 1) * N_OUT], in_=result[:])

        def keep_clock(rows):
            unread = sum_psum.tile([P, N_OUT], F32, name="unread", tag="total")
            nc.tensor.matmul(unread[:], lhsT=blank[:, 0:P], rhs=rows, start=True, stop=True)

        for i in range(4):
            keep_clock(blank[:])
        keep_clock(h_rows[0][:, 0:N_OUT])
        keep_clock(h_rows[0][:, N_OUT:H])
        make_y(0)
        flip_y(0)
        keep_clock(h_rows[1][:, 0:N_OUT])
        make_y(1)
        flip_y(1)
        keep_clock(h_rows[2][:, 0:N_OUT])
        make_y(2)
        flip_y(2)
        spread_b1()
        keep_clock(h_rows[3][:, 0:N_OUT])
        make_y(3)
        pack_y(0)
        pack_y(1)
        flip_w1(0)
        flip_y(3)
        keep_clock(blank[:])
        pack_y(2)
        flip_w1(1)
        keep_clock(blank[:])
        pack_w1(0)
        pack_y(3)
        flip_w1(2)
        keep_clock(blank[:])
        pack_w1(1)
        flip_w1(3)
        pack_w1(2)
        pack_w1(3)
        layer_1(0)
        flip_w2(0)
        flip_w2(1)
        for c in range(1, CHUNKS):
            layer_1(c)
        pack_w2(0)
        group_z(0)
        pack_w2(1)
        pack_z(0)
        flip_w2(2)
        flip_w2(3)
        first_range = [new_total() for t in range(B_TILES)]
        for t in range(B_TILES):
            layer_2_pass(first_range[t], 0, t, 0)
        group_z(1)
        pack_z(1)
        pack_w2(2)
        pack_w2(3)
        for t in range(B_TILES):
            layer_2_pass(first_range[t], 0, t, 1)
            finish(first_range[t], 0, t)
        for t in range(B_TILES):
            total = new_total()
            for g in range(PASSES):
                layer_2_pass(total, 1, t, g)
            finish(total, 1, t)
